import numpy as np
import ml_dtypes


def mxq(x, axis, fmt="e4m3"):
    dtype, down = {"e4m3": (ml_dtypes.float8_e4m3fn, 7), "e5m2": (ml_dtypes.float8_e5m2, 14)}[fmt]
    v = np.moveaxis(np.asarray(x, np.float32).astype(ml_dtypes.bfloat16).astype(np.float64), axis, -1)
    blocks = v.reshape(v.shape[:-1] + (-1, 32))
    amax = np.abs(blocks).max(-1, keepdims=True)
    byte = np.maximum(np.where(amax > 0, np.frexp(amax)[1] - 1 + 127, 0) - down, 1)
    scale = np.exp2(byte - 127.0)
    codes = (blocks / scale).astype(np.float32).astype(dtype).astype(np.float64)
    return np.moveaxis((codes * scale).reshape(v.shape), -1, axis)


WIDE = False


def mx_kscale(k):
    if not WIDE:
        return np.ones(k)
    levels = np.array([20, -20, 10, -10, 0])
    a = np.random.permutation(np.resize(levels, k // 512 * 4)).reshape(k // 512, 4)
    idx = np.arange(k)
    return np.exp2(a[idx // 512, idx % 128 // 32])


BF16 = ml_dtypes.bfloat16


def bf(x):
    return np.asarray(x, np.float32).astype(BF16)


def f64(x):
    return np.asarray(x).astype(np.float64)


B, S, IN, OUT, SP = 4, 512, 512, 4096, 512


def setup_inputs():
    u = mx_kscale(OUT)
    x = np.random.standard_normal((B, S, IN))
    weights = np.random.standard_normal((OUT, IN)) / np.sqrt(IN) / u[:, None]
    g = np.random.standard_normal((B, S, OUT)) * np.exp2(np.random.randint(-12, 1, (B, S, 1))) * 8.0 * u
    return {"x": bf(x), "weights": bf(weights), "grad_out": bf(g)}


def reference(x, weights, grad_out):
    weights = f64(weights)
    g = f64(grad_out).reshape(-1, OUT)
    g_sparse = g[:, :SP]
    g_dense = g[:, SP:]
    w_sparse = weights[:SP, :]
    w_dense = weights[SP:, :]
    gx_sparse = mxq(g_sparse, 1, "e5m2") @ mxq(w_sparse, 0, "e4m3")
    gx_dense = mxq(g_dense, 1, "e5m2") @ mxq(w_dense, 0, "e4m3")
    return (gx_sparse + gx_dense).reshape(B, S, IN)

@@ -1,0 +1,194 @@
+import concourse.mybir as mybir
+from concourse.masks import make_identity
+
+F32 = mybir.dt.float32
+BF16 = mybir.dt.bfloat16
+U32 = mybir.dt.uint32
+U8 = mybir.dt.uint8
+E5M2X4 = mybir.dt.float8_e5m2_x4
+E4M3X4 = mybir.dt.float8_e4m3fn_x4
+
+P = 128
+TOKENS = 2048
+K = 4096
+N = 512
+K_PASS = 512
+PASSES = K // K_PASS
+TILES = TOKENS // P
+WORDS = K_PASS // 2
+HEAD = 4
+W_VECTOR_GROUPS = 80
+
+FLOPS = 2 * TOKENS * K * N
+BYTES = 2 * TOKENS * K + 2 * K * N + 4 * TOKENS * N
+
+
+def tile_myinterleavedmodule_t_kernel(tc, x, weights, grad_out, out):
+    nc = tc.nc
+    g = grad_out.flatten_outer_dims().rearrange("(p i) k -> p i k", i=TILES)
+    o = out.flatten_outer_dims().rearrange("(p i) n -> p i n", i=TILES)
+
+    with tc.tile_pool(name="const", bufs=1) as const, \
+            tc.tile_pool(name="raw", bufs=1) as raw, \
+            tc.tile_pool(name="wwork", bufs=2) as wwork, \
+            tc.tile_pool(name="gwork", bufs=4) as gwork, \
+            tc.tile_pool(name="gq", bufs=6) as gq, \
+            tc.tile_pool(name="stage", bufs=4) as stage, \
+            tc.psum_pool(name="psum", bufs=1) as psum, \
+            tc.manual_schedule():
+
+        src = {}
+        w_raw = {}
+        w_codes = {}
+        w_scales = {}
+        acc = {}
+        ready = {}
+        tp_next = [0]
+
+        def copy(engine, dst, source):
+            if engine == "v":
+                nc.vector.tensor_copy(out=dst, in_=source)
+            else:
+                nc.scalar.copy(out=dst, in_=source)
+
+        def load_head(c0, n):
+            t = raw.tile([P, HEAD * n * K_PASS], BF16, name="g_head%d" % c0)
+            nc.sync.dma_start(
+                out=t[:].rearrange("p (i k) -> p i k", i=HEAD),
+                in_=g[:, 0:HEAD, c0 * K_PASS:(c0 + n) * K_PASS],
+            )
+            words = t[:].bitcast(F32)
+            for i in range(HEAD):
+                for c in range(c0, c0 + n):
+                    base = (i * n + c - c0) * WORDS
+                    src[(i, c)] = words[:, base:base + WORDS]
+
+        def load_tile(i):
+            t = raw.tile([P, K], BF16, name="g_tile%d" % i)
+            nc.sync.dma_start(out=t[:], in_=g[:, i, :])
+            words = t[:].bitcast(F32)
+            for c in range(PASSES):
+                src[(i, c)] = words[:, c * WORDS:(c + 1) * WORDS]
+
+        def load_w(c):
+            t = raw.tile([P, 4 * N], BF16, name="w_raw%d" % c)
+            nc.sync.dma_start(
+                out=t[:].rearrange("p (u e n) -> p u e n", u=2, e=2),
+                in_=weights[c * K_PASS:(c + 1) * K_PASS, :].rearrange("(u p e) n -> p u e n", u=2, e=2),
+            )
+            w_raw[c] = t
+
+        def transpose_chunk(ops):
+            banks = []
+            for b in range(len(ops) // 2):
+                bank = psum.tile([P, 512], F32, name="tp", tag="bank%d" % (HEAD + tp_next[0] % 4))
+                tp_next[0] += 1
+                for j in range(2):
+                    words = src[ops[2 * b + j]]
+                    for u in range(2):
+                        s = 2 * j + u
+                        nc.tensor.transpose(bank[:, s * P:(s + 1) * P], words[:, u * P:(u + 1) * P], ident[:])
+                banks.append(bank)
+            return banks
+
+        def copy_chunk(banks, engines):
+            grp = gwork.tile([P, 4 * K_PASS], BF16, name="grp", align_bytes=64)
+            grp_words = grp[:].bitcast(F32)
+            for b, bank in enumerate(banks):
+                copy(
+                    engines[b],
+                    grp_words[:, b * 512:(b + 1) * 512].rearrange("p (o r u) -> p o r u", o=2, u=2),
+                    bank[:].rearrange("p (o u r) -> p o r u", o=2, u=2),
+                )
+            return grp
+
+        def quantise_chunk(grp):
+            codes = gq.tile([P, 4 * P], U32, name="g_codes", align_bytes=64)
+            scales = gq.tile([P, 4 * P], U8, name="g_scales", align_bytes=64)
+            nc.vector.quantize_mx(out=codes[:].bitcast(E5M2X4), scales=scales[:], in_=grp[:])
+            return codes, scales
+
+        def regroup_w(c):
+            grp = wwork.tile([P, 4 * N], BF16, name="w_grp", align_bytes=64)
+            dst = grp[:].rearrange("p (c i t) -> p c t i", i=4, t=4)
+            source = w_raw[c][:].rearrange("p (t c i) -> p c t i", t=4, i=4)
+            v = W_VECTOR_GROUPS
+            nc.vector.tensor_copy(out=dst[:, 0:v], in_=source[:, 0:v])
+            nc.scalar.copy(out=dst[:, v:], in_=source[:, v:])
+            return grp
+
+        def quantise_w(c, grp):
+            w_codes[c] = const.tile([P, N], U32, name="w_codes%d" % c, align_bytes=64)
+            w_scales[c] = const.tile([P, N], U8, name="w_scales%d" % c, align_bytes=64)
+            nc.vector.quantize_mx(out=w_codes[c][:].bitcast(E4M3X4), scales=w_scales[c][:], in_=grp[:])
+
+        def multiply_chunk(ops, codes, scales):
+            for j, (i, c) in enumerate(ops):
+                if c == 0:
+                    acc[i] = psum.tile([P, N], F32, name="acc", tag="bank%d" % (i % HEAD))
+                nc.tensor.matmul_mx(
+                    out=acc[i][:],
+                    lhsT=codes[:, j * P:(j + 1) * P].bitcast(E5M2X4),
+                    lhsT_scale=scales[:, j * P:(j + 1) * P],
+                    rhs=w_codes[c][:].bitcast(E4M3X4),
+                    rhs_scale=w_scales[c][:],
+                    start=(c == 0),
+                    stop=(c == PASSES - 1),
+                )
+
+        def finish(i, engine):
+            res = stage.tile([P, N], F32, name="res")
+            copy(engine, res[:], acc[i][:])
+            nc.sync.dma_start(out=o[:, i, :], in_=res[:])
+
+        def prepare_head(c):
+            ops = [(i, c) for i in range(HEAD)]
+            banks = transpose_chunk(ops)
+            grp = copy_chunk(banks, "ss")
+            w_grp = regroup_w(c)
+            codes, scales = quantise_chunk(grp)
+            quantise_w(c, w_grp)
+            ready[c] = [(ops, codes, scales)]
+
+        def prepare_tile(i):
+            halves = [[(i, c) for c in range(0, 4)], [(i, c) for c in range(4, 8)]]
+            banks = [transpose_chunk(ops) for ops in halves]
+            grps = [copy_chunk(banks[0], "ss"), copy_chunk(banks[1], "sv")]
+            ready[PASSES + i] = [(halves[h],) + quantise_chunk(grps[h]) for h in range(2)]
+
+        def multiply(key):
+            for ops, codes, scales in ready[key]:
+                multiply_chunk(ops, codes, scales)
+
+        ident = const.tile([P, P], F32, name="ident")
+        make_identity(nc, ident[:])
+
+        load_head(0, 1)
+        load_w(0)
+        load_head(1, 1)
+        load_w(1)
+        for c0 in (2, 4, 6):
+            load_head(c0, 2)
+            load_w(c0)
+            load_w(c0 + 1)
+        for i in range(HEAD, TILES):
+            load_tile(i)
+
+        prepare_head(0)
+        prepare_head(1)
+        multiply(0)
+        for c0 in (2, 4, 6):
+            prepare_head(c0)
+            prepare_head(c0 + 1)
+            multiply(c0 - 1)
+            multiply(c0)
+        prepare_tile(HEAD)
+        multiply(PASSES - 1)
+        for i in range(HEAD):
+            finish(i, "sv"[i % 2])
+        for i in range(HEAD + 1, TILES):
+            prepare_tile(i)
+            multiply(PASSES + i - 1)
+            finish(i - 1, "s")
+        multiply(PASSES + TILES - 1)
+        finish(TILES - 1, "v")

@@ -18,6 +18,7 @@ TILES = TOKENS // P
 WORDS = K_PASS // 2
 HEAD = 4
 W_VECTOR_GROUPS = 80
+RING = 6
 
 FLOPS = 2 * TOKENS * K * N
 BYTES = 2 * TOKENS * K + 2 * K * N + 4 * TOKENS * N
@@ -33,7 +34,8 @@ def tile_myinterleavedmodule_t_kernel(tc, x, weights, grad_out, out):
             tc.tile_pool(name="wwork", bufs=2) as wwork, \
             tc.tile_pool(name="gwork", bufs=4) as gwork, \
             tc.tile_pool(name="gq", bufs=6) as gq, \
-            tc.tile_pool(name="stage", bufs=4) as stage, \
+            tc.tile_pool(name="stage", bufs=8) as stage, \
+            tc.tile_pool(name="gring", bufs=RING) as gring, \
             tc.psum_pool(name="psum", bufs=1) as psum, \
             tc.manual_schedule():
 
@@ -64,7 +66,7 @@ def tile_myinterleavedmodule_t_kernel(tc, x, weights, grad_out, out):
                     src[(i, c)] = words[:, base:base + WORDS]
 
         def load_tile(i):
-            t = raw.tile([P, K], BF16, name="g_tile%d" % i)
+            t = gring.tile([P, K], BF16, name="g_tile")
             nc.sync.dma_start(out=t[:], in_=g[:, i, :])
             words = t[:].bitcast(F32)
             for c in range(PASSES):
@@ -171,7 +173,7 @@ def tile_myinterleavedmodule_t_kernel(tc, x, weights, grad_out, out):
             load_head(c0, 2)
             load_w(c0)
             load_w(c0 + 1)
-        for i in range(HEAD, TILES):
+        for i in range(HEAD, HEAD + RING):
             load_tile(i)
 
         prepare_head(0)
@@ -183,11 +185,14 @@ def tile_myinterleavedmodule_t_kernel(tc, x, weights, grad_out, out):
             multiply(c0 - 1)
             multiply(c0)
         prepare_tile(HEAD)
+        load_tile(HEAD + RING)
         multiply(PASSES - 1)
         for i in range(HEAD):
             finish(i, "sv"[i % 2])
         for i in range(HEAD + 1, TILES):
             prepare_tile(i)
+            if i + RING < TILES:
+                load_tile(i + RING)
             multiply(PASSES + i - 1)
             finish(i - 1, "s")
         multiply(PASSES + TILES - 1)

@@ -19,6 +19,7 @@ WORDS = K_PASS // 2
 HEAD = 4
 W_VECTOR_GROUPS = 80
 RING = 6
+GROUP_TILES = [1,1,2,2,2,2,2]
 
 FLOPS = 2 * TOKENS * K * N
 BYTES = 2 * TOKENS * K + 2 * K * N + 4 * TOKENS * N
@@ -32,8 +33,8 @@ def tile_myinterleavedmodule_t_kernel(tc, x, weights, grad_out, out):
     with tc.tile_pool(name="const", bufs=1) as const, \
             tc.tile_pool(name="raw", bufs=1) as raw, \
             tc.tile_pool(name="wwork", bufs=2) as wwork, \
-            tc.tile_pool(name="gwork", bufs=4) as gwork, \
-            tc.tile_pool(name="gq", bufs=6) as gq, \
+            tc.tile_pool(name="gwork", bufs=6) as gwork, \
+            tc.tile_pool(name="gq", bufs=12) as gq, \
             tc.tile_pool(name="stage", bufs=8) as stage, \
             tc.tile_pool(name="gring", bufs=RING) as gring, \
             tc.psum_pool(name="psum", bufs=1) as psum, \
@@ -44,7 +45,6 @@ def tile_myinterleavedmodule_t_kernel(tc, x, weights, grad_out, out):
         w_codes = {}
         w_scales = {}
         acc = {}
-        ready = {}
         tp_next = [0]
 
         def copy(engine, dst, source):
@@ -80,9 +80,10 @@ def tile_myinterleavedmodule_t_kernel(tc, x, weights, grad_out, out):
             )
             w_raw[c] = t
 
-        def transpose_chunk(ops):
-            banks = []
-            for b in range(len(ops) // 2):
+        def transpose_and_copy(ops, engines):
+            grp = gwork.tile([P, 4 * K_PASS], BF16, name="grp", align_bytes=64)
+            grp_words = grp[:].bitcast(F32)
+            for b in range(2):
                 bank = psum.tile([P, 512], F32, name="tp", tag="bank%d" % (HEAD + tp_next[0] % 4))
                 tp_next[0] += 1
                 for j in range(2):
@@ -90,13 +91,6 @@ def tile_myinterleavedmodule_t_kernel(tc, x, weights, grad_out, out):
                     for u in range(2):
                         s = 2 * j + u
                         nc.tensor.transpose(bank[:, s * P:(s + 1) * P], words[:, u * P:(u + 1) * P], ident[:])
-                banks.append(bank)
-            return banks
-
-        def copy_chunk(banks, engines):
-            grp = gwork.tile([P, 4 * K_PASS], BF16, name="grp", align_bytes=64)
-            grp_words = grp[:].bitcast(F32)
-            for b, bank in enumerate(banks):
                 copy(
                     engines[b],
                     grp_words[:, b * 512:(b + 1) * 512].rearrange("p (o r u) -> p o r u", o=2, u=2),
@@ -124,43 +118,40 @@ def tile_myinterleavedmodule_t_kernel(tc, x, weights, grad_out, out):
             w_scales[c] = const.tile([P, N], U8, name="w_scales%d" % c, align_bytes=64)
             nc.vector.quantize_mx(out=w_codes[c][:].bitcast(E4M3X4), scales=w_scales[c][:], in_=grp[:])
 
-        def multiply_chunk(ops, codes, scales):
-            for j, (i, c) in enumerate(ops):
-                if c == 0:
-                    acc[i] = psum.tile([P, N], F32, name="acc", tag="bank%d" % (i % HEAD))
-                nc.tensor.matmul_mx(
-                    out=acc[i][:],
-                    lhsT=codes[:, j * P:(j + 1) * P].bitcast(E5M2X4),
-                    lhsT_scale=scales[:, j * P:(j + 1) * P],
-                    rhs=w_codes[c][:].bitcast(E4M3X4),
-                    rhs_scale=w_scales[c][:],
-                    start=(c == 0),
-                    stop=(c == PASSES - 1),
-                )
-
         def finish(i, engine):
             res = stage.tile([P, N], F32, name="res")
             copy(engine, res[:], acc[i][:])
             nc.sync.dma_start(out=o[:, i, :], in_=res[:])
 
+        def multiply(group):
+            for ops, codes, scales in group:
+                for j, (i, c) in enumerate(ops):
+                    if c == 0:
+                        acc[i] = psum.tile([P, N], F32, name="acc", tag="bank%d" % (i % HEAD))
+                    nc.tensor.matmul_mx(
+                        out=acc[i][:],
+                        lhsT=codes[:, j * P:(j + 1) * P].bitcast(E5M2X4),
+                        lhsT_scale=scales[:, j * P:(j + 1) * P],
+                        rhs=w_codes[c][:].bitcast(E4M3X4),
+                        rhs_scale=w_scales[c][:],
+                        start=(c == 0),
+                        stop=(c == PASSES - 1),
+                    )
+                    if c == PASSES - 1:
+                        finish(i, "sv"[i % 2] if i < HEAD else ("v" if i == TILES - 1 else "s"))
+
         def prepare_head(c):
             ops = [(i, c) for i in range(HEAD)]
-            banks = transpose_chunk(ops)
-            grp = copy_chunk(banks, "ss")
+            grp = transpose_and_copy(ops, "ss")
             w_grp = regroup_w(c)
             codes, scales = quantise_chunk(grp)
             quantise_w(c, w_grp)
-            ready[c] = [(ops, codes, scales)]
+            return [(ops, codes, scales)]
 
-        def prepare_tile(i):
-            halves = [[(i, c) for c in range(0, 4)], [(i, c) for c in range(4, 8)]]
-            banks = [transpose_chunk(ops) for ops in halves]
-            grps = [copy_chunk(banks[0], "ss"), copy_chunk(banks[1], "sv")]
-            ready[PASSES + i] = [(halves[h],) + quantise_chunk(grps[h]) for h in range(2)]
-
-        def multiply(key):
-            for ops, codes, scales in ready[key]:
-                multiply_chunk(ops, codes, scales)
+        def prepare_tiles(tiles):
+            chunks = [[(i, c) for c in range(h, h + 4)] for i in tiles for h in (0, 4)]
+            grps = [transpose_and_copy(ops, "sv") for ops in chunks]
+            return [(ops,) + quantise_chunk(grp) for ops, grp in zip(chunks, grps)]
 
         ident = const.tile([P, P], F32, name="ident")
         make_identity(nc, ident[:])
@@ -175,25 +166,23 @@ def tile_myinterleavedmodule_t_kernel(tc, x, weights, grad_out, out):
             load_w(c0 + 1)
         for i in range(HEAD, HEAD + RING):
             load_tile(i)
+        loaded = HEAD + RING
 
-        prepare_head(0)
-        prepare_head(1)
-        multiply(0)
+        head = {0: prepare_head(0), 1: prepare_head(1)}
+        multiply(head[0])
         for c0 in (2, 4, 6):
-            prepare_head(c0)
-            prepare_head(c0 + 1)
-            multiply(c0 - 1)
-            multiply(c0)
-        prepare_tile(HEAD)
-        load_tile(HEAD + RING)
-        multiply(PASSES - 1)
-        for i in range(HEAD):
-            finish(i, "sv"[i % 2])
-        for i in range(HEAD + 1, TILES):
-            prepare_tile(i)
-            if i + RING < TILES:
-                load_tile(i + RING)
-            multiply(PASSES + i - 1)
-            finish(i - 1, "s")
-        multiply(PASSES + TILES - 1)
-        finish(TILES - 1, "v")
+            head[c0] = prepare_head(c0)
+            head[c0 + 1] = prepare_head(c0 + 1)
+            multiply(head[c0 - 1])
+            multiply(head[c0])
+        pending = head[PASSES - 1]
+        first = HEAD
+        for count in GROUP_TILES:
+            following = prepare_tiles(list(range(first, first + count)))
+            first += count
+            for i in range(loaded, min(loaded + count, TILES)):
+                load_tile(i)
+            loaded = min(loaded + count, TILES)
+            multiply(pending)
+            pending = following
+        multiply(pending)

@@ -7,6 +7,7 @@ U32 = mybir.dt.uint32
 U8 = mybir.dt.uint8
 E5M2X4 = mybir.dt.float8_e5m2_x4
 E4M3X4 = mybir.dt.float8_e4m3fn_x4
+ADD = mybir.AluOpType.add
 
 P = 128
 TOKENS = 2048
@@ -14,12 +15,13 @@ K = 4096
 N = 512
 K_PASS = 512
 PASSES = K // K_PASS
+HALF = PASSES // 2
 TILES = TOKENS // P
 WORDS = K_PASS // 2
 HEAD = 4
 W_VECTOR_GROUPS = 80
 RING = 6
-GROUP_TILES = [1,1,2,2,2,2,2]
+PAIR = 2
 
 FLOPS = 2 * TOKENS * K * N
 BYTES = 2 * TOKENS * K + 2 * K * N + 4 * TOKENS * N
@@ -33,9 +35,8 @@ def tile_myinterleavedmodule_t_kernel(tc, x, weights, grad_out, out):
     with tc.tile_pool(name="const", bufs=1) as const, \
             tc.tile_pool(name="raw", bufs=1) as raw, \
             tc.tile_pool(name="wwork", bufs=2) as wwork, \
-            tc.tile_pool(name="gwork", bufs=6) as gwork, \
-            tc.tile_pool(name="gq", bufs=12) as gq, \
-            tc.tile_pool(name="stage", bufs=8) as stage, \
+            tc.tile_pool(name="gwork", bufs=4) as gwork, \
+            tc.tile_pool(name="gq", bufs=6) as gq, \
             tc.tile_pool(name="gring", bufs=RING) as gring, \
             tc.psum_pool(name="psum", bufs=1) as psum, \
             tc.manual_schedule():
@@ -45,7 +46,9 @@ def tile_myinterleavedmodule_t_kernel(tc, x, weights, grad_out, out):
         w_codes = {}
         w_scales = {}
         acc = {}
+        part = {}
         tp_next = [0]
+        acc_next = [0]
 
         def copy(engine, dst, source):
             if engine == "v":
@@ -53,24 +56,28 @@ def tile_myinterleavedmodule_t_kernel(tc, x, weights, grad_out, out):
             else:
                 nc.scalar.copy(out=dst, in_=source)
 
-        def load_head(c0, n):
-            t = raw.tile([P, HEAD * n * K_PASS], BF16, name="g_head%d" % c0)
+        def load_head(c):
+            t = raw.tile([P, HEAD * K_PASS], BF16, name="g_head%d" % c)
             nc.sync.dma_start(
                 out=t[:].rearrange("p (i k) -> p i k", i=HEAD),
-                in_=g[:, 0:HEAD, c0 * K_PASS:(c0 + n) * K_PASS],
+                in_=g[:, 0:HEAD, c * K_PASS:(c + 1) * K_PASS],
             )
             words = t[:].bitcast(F32)
             for i in range(HEAD):
-                for c in range(c0, c0 + n):
-                    base = (i * n + c - c0) * WORDS
-                    src[(i, c)] = words[:, base:base + WORDS]
+                src[(i, c)] = words[:, i * WORDS:(i + 1) * WORDS]
 
-        def load_tile(i):
-            t = gring.tile([P, K], BF16, name="g_tile")
-            nc.sync.dma_start(out=t[:], in_=g[:, i, :])
+        def load_pair(first, half):
+            t = gring.tile([P, PAIR * HALF * K_PASS], BF16, name="g_pair")
+            k0 = half * HALF * K_PASS
+            nc.sync.dma_start(
+                out=t[:].rearrange("p (i k) -> p i k", i=PAIR),
+                in_=g[:, first:first + PAIR, k0:k0 + HALF * K_PASS],
+            )
             words = t[:].bitcast(F32)
-            for c in range(PASSES):
-                src[(i, c)] = words[:, c * WORDS:(c + 1) * WORDS]
+            for j in range(PAIR):
+                for c in range(HALF):
+                    base = (j * HALF + c) * WORDS
+                    src[(first + j, half * HALF + c)] = words[:, base:base + WORDS]
 
         def load_w(c):
             t = raw.tile([P, 4 * N], BF16, name="w_raw%d" % c)
@@ -118,27 +125,27 @@ def tile_myinterleavedmodule_t_kernel(tc, x, weights, grad_out, out):
             w_scales[c] = const.tile([P, N], U8, name="w_scales%d" % c, align_bytes=64)
             nc.vector.quantize_mx(out=w_codes[c][:].bitcast(E4M3X4), scales=w_scales[c][:], in_=grp[:])
 
-        def finish(i, engine):
-            res = stage.tile([P, N], F32, name="res")
-            copy(engine, res[:], acc[i][:])
-            nc.sync.dma_start(out=o[:, i, :], in_=res[:])
-
         def multiply(group):
             for ops, codes, scales in group:
                 for j, (i, c) in enumerate(ops):
-                    if c == 0:
-                        acc[i] = psum.tile([P, N], F32, name="acc", tag="bank%d" % (i % HEAD))
+                    if c % HALF == 0:
+                        acc[i] = psum.tile([P, N], F32, name="acc", tag="bank%d" % (acc_next[0] % HEAD))
+                        acc_next[0] += 1
                     nc.tensor.matmul_mx(
                         out=acc[i][:],
                         lhsT=codes[:, j * P:(j + 1) * P].bitcast(E5M2X4),
                         lhsT_scale=scales[:, j * P:(j + 1) * P],
                         rhs=w_codes[c][:].bitcast(E4M3X4),
                         rhs_scale=w_scales[c][:],
-                        start=(c == 0),
-                        stop=(c == PASSES - 1),
+                        start=(c % HALF == 0),
+                        stop=(c % HALF == HALF - 1),
                     )
+                    if c == HALF - 1:
+                        part[i] = const.tile([P, N], F32, name="part%d" % i)
+                        nc.scalar.copy(out=part[i][:], in_=acc[i][:])
                     if c == PASSES - 1:
-                        finish(i, "sv"[i % 2] if i < HEAD else ("v" if i == TILES - 1 else "s"))
+                        nc.vector.tensor_tensor(out=part[i][:], in0=acc[i][:], in1=part[i][:], op=ADD)
+                        nc.sync.dma_start(out=o[:, i, :], in_=part[i][:])
 
         def prepare_head(c):
             ops = [(i, c) for i in range(HEAD)]
@@ -148,41 +155,41 @@ def tile_myinterleavedmodule_t_kernel(tc, x, weights, grad_out, out):
             quantise_w(c, w_grp)
             return [(ops, codes, scales)]
 
-        def prepare_tiles(tiles):
-            chunks = [[(i, c) for c in range(h, h + 4)] for i in tiles for h in (0, 4)]
-            grps = [transpose_and_copy(ops, "sv") for ops in chunks]
-            return [(ops,) + quantise_chunk(grp) for ops, grp in zip(chunks, grps)]
+        def prepare_pair(first, half, w_chunk):
+            chunks = [[(i, half * HALF + c) for c in range(HALF)] for i in range(first, first + PAIR)]
+            grps = [transpose_and_copy(chunks[0], "ss"), transpose_and_copy(chunks[1], "sv")]
+            w_grp = regroup_w(w_chunk) if w_chunk is not None else None
+            group = [(ops,) + quantise_chunk(grp) for ops, grp in zip(chunks, grps)]
+            if w_chunk is not None:
+                quantise_w(w_chunk, w_grp)
+            return group
 
         ident = const.tile([P, P], F32, name="ident")
         make_identity(nc, ident[:])
 
-        load_head(0, 1)
-        load_w(0)
-        load_head(1, 1)
-        load_w(1)
-        for c0 in (2, 4, 6):
-            load_head(c0, 2)
-            load_w(c0)
-            load_w(c0 + 1)
-        for i in range(HEAD, HEAD + RING):
-            load_tile(i)
-        loaded = HEAD + RING
+        pairs = [(first, 0) for first in range(HEAD, TILES, PAIR)] + [(first, 1) for first in range(0, TILES, PAIR)]
+        late_w_after = {1: 4, 2: 5, 3: 6, 4: 7}
 
-        head = {0: prepare_head(0), 1: prepare_head(1)}
-        multiply(head[0])
-        for c0 in (2, 4, 6):
-            head[c0] = prepare_head(c0)
-            head[c0 + 1] = prepare_head(c0 + 1)
-            multiply(head[c0 - 1])
-            multiply(head[c0])
-        pending = head[PASSES - 1]
-        first = HEAD
-        for count in GROUP_TILES:
-            following = prepare_tiles(list(range(first, first + count)))
-            first += count
-            for i in range(loaded, min(loaded + count, TILES)):
-                load_tile(i)
-            loaded = min(loaded + count, TILES)
+        def load_next(n):
+            if n < len(pairs):
+                load_pair(pairs[n][0], pairs[n][1])
+                if n in late_w_after:
+                    load_w(late_w_after[n])
+
+        for c in range(HALF):
+            load_head(c)
+            load_w(c)
+        for n in range(RING):
+            load_next(n)
+
+        pending = prepare_head(0)
+        for c in range(1, HALF):
+            following = prepare_head(c)
+            multiply(pending)
+            pending = following
+        for n, (first, half) in enumerate(pairs):
+            following = prepare_pair(first, half, late_w_after.get(n - 1))
+            load_next(n + RING)
             multiply(pending)
             pending = following
         multiply(pending)

@@ -66,13 +66,18 @@ def tile_myinterleavedmodule_t_kernel(tc, x, weights, grad_out, out):
             for i in range(HEAD):
                 src[(i, c)] = words[:, i * WORDS:(i + 1) * WORDS]
 
-        def load_pair(first, half):
+        def load_pair(first, half, split):
             t = gring.tile([P, PAIR * HALF * K_PASS], BF16, name="g_pair")
             k0 = half * HALF * K_PASS
-            nc.sync.dma_start(
-                out=t[:].rearrange("p (i k) -> p i k", i=PAIR),
-                in_=g[:, first:first + PAIR, k0:k0 + HALF * K_PASS],
-            )
+            width = HALF * K_PASS
+            if split:
+                for j in range(PAIR):
+                    nc.sync.dma_start(out=t[:, j * width:(j + 1) * width], in_=g[:, first + j, k0:k0 + width])
+            else:
+                nc.sync.dma_start(
+                    out=t[:].rearrange("p (i k) -> p i k", i=PAIR),
+                    in_=g[:, first:first + PAIR, k0:k0 + width],
+                )
             words = t[:].bitcast(F32)
             for j in range(PAIR):
                 for c in range(HALF):
@@ -168,11 +173,11 @@ def tile_myinterleavedmodule_t_kernel(tc, x, weights, grad_out, out):
         make_identity(nc, ident[:])
 
         pairs = [(first, 0) for first in range(HEAD, TILES, PAIR)] + [(first, 1) for first in range(0, TILES, PAIR)]
-        late_w_after = {1: 4, 2: 5, 3: 6, 4: 7}
+        late_w_after = {2: 4, 3: 5, 4: 6, 5: 7}
 
         def load_next(n):
             if n < len(pairs):
-                load_pair(pairs[n][0], pairs[n][1])
+                load_pair(pairs[n][0], pairs[n][1], n < 2)
                 if n in late_w_after:
                     load_w(late_w_after[n])
 

@@ -22,6 +22,7 @@ HEAD = 4
 W_VECTOR_GROUPS = 80
 RING = 6
 PAIR = 2
+WARM = (6, 4, 2)
 
 FLOPS = 2 * TOKENS * K * N
 BYTES = 2 * TOKENS * K + 2 * K * N + 4 * TOKENS * N
@@ -152,9 +153,16 @@ def tile_myinterleavedmodule_t_kernel(tc, x, weights, grad_out, out):
                         nc.vector.tensor_tensor(out=part[i][:], in0=acc[i][:], in1=part[i][:], op=ADD)
                         nc.sync.dma_start(out=o[:, i, :], in_=part[i][:])
 
+        def keep_warm(count):
+            for n in range(count):
+                bank = psum.tile([P, 512], F32, name="warm", tag="bank0")
+                nc.tensor.matmul(bank[:], lhsT=zeros[:, 0:P], rhs=zeros[:], start=True, stop=True)
+
         def prepare_head(c):
             ops = [(i, c) for i in range(HEAD)]
             grp = transpose_and_copy(ops, "ss")
+            if c < len(WARM) - 1:
+                keep_warm(WARM[c + 1])
             w_grp = regroup_w(c)
             codes, scales = quantise_chunk(grp)
             quantise_w(c, w_grp)
@@ -171,6 +179,8 @@ def tile_myinterleavedmodule_t_kernel(tc, x, weights, grad_out, out):
 
         ident = const.tile([P, P], F32, name="ident")
         make_identity(nc, ident[:])
+        zeros = const.tile([P, 512], BF16, name="zeros")
+        nc.vector.memset(zeros[:], 0.0)
 
         pairs = [(first, 0) for first in range(HEAD, TILES, PAIR)] + [(first, 1) for first in range(0, TILES, PAIR)]
         late_w_after = {2: 4, 3: 5, 4: 6, 5: 7}
@@ -187,6 +197,7 @@ def tile_myinterleavedmodule_t_kernel(tc, x, weights, grad_out, out):
         for n in range(RING):
             load_next(n)
 
+        keep_warm(WARM[0])
         pending = prepare_head(0)
         for c in range(1, HALF):
             following = prepare_head(c)

@@ -22,7 +22,10 @@ HEAD = 4
 W_VECTOR_GROUPS = 80
 RING = 6
 PAIR = 2
-WARM = (6, 4, 2)
+HELD = (12, 13, 14, 15)
+PART_V = ()
+LAST = 11
+WARM = (4, 3, 0)
 
 FLOPS = 2 * TOKENS * K * N
 BYTES = 2 * TOKENS * K + 2 * K * N + 4 * TOKENS * N
@@ -36,8 +39,8 @@ def tile_myinterleavedmodule_t_kernel(tc, x, weights, grad_out, out):
     with tc.tile_pool(name="const", bufs=1) as const, \
             tc.tile_pool(name="raw", bufs=1) as raw, \
             tc.tile_pool(name="wwork", bufs=2) as wwork, \
-            tc.tile_pool(name="gwork", bufs=4) as gwork, \
-            tc.tile_pool(name="gq", bufs=6) as gq, \
+            tc.tile_pool(name="gwork", bufs=6) as gwork, \
+            tc.tile_pool(name="gq", bufs=9) as gq, \
             tc.tile_pool(name="gring", bufs=RING) as gring, \
             tc.psum_pool(name="psum", bufs=1) as psum, \
             tc.manual_schedule():
@@ -59,10 +62,13 @@ def tile_myinterleavedmodule_t_kernel(tc, x, weights, grad_out, out):
 
         def load_head(c):
             t = raw.tile([P, HEAD * K_PASS], BF16, name="g_head%d" % c)
-            nc.sync.dma_start(
-                out=t[:].rearrange("p (i k) -> p i k", i=HEAD),
-                in_=g[:, 0:HEAD, c * K_PASS:(c + 1) * K_PASS],
-            )
+            view = t[:].rearrange("p (i k) -> p i k", i=HEAD)
+            step = HEAD // 2 if c == 0 else HEAD
+            for j in range(0, HEAD, step):
+                nc.sync.dma_start(
+                    out=view[:, j:j + step],
+                    in_=g[:, j:j + step, c * K_PASS:(c + 1) * K_PASS],
+                )
             words = t[:].bitcast(F32)
             for i in range(HEAD):
                 src[(i, c)] = words[:, i * WORDS:(i + 1) * WORDS]
@@ -93,29 +99,39 @@ def tile_myinterleavedmodule_t_kernel(tc, x, weights, grad_out, out):
             )
             w_raw[c] = t
 
-        def transpose_and_copy(ops, engines):
-            grp = gwork.tile([P, 4 * K_PASS], BF16, name="grp", align_bytes=64)
-            grp_words = grp[:].bitcast(F32)
-            for b in range(2):
-                bank = psum.tile([P, 512], F32, name="tp", tag="bank%d" % (HEAD + tp_next[0] % 4))
-                tp_next[0] += 1
-                for j in range(2):
-                    words = src[ops[2 * b + j]]
-                    for u in range(2):
-                        s = 2 * j + u
-                        nc.tensor.transpose(bank[:, s * P:(s + 1) * P], words[:, u * P:(u + 1) * P], ident[:])
-                copy(
-                    engines[b],
-                    grp_words[:, b * 512:(b + 1) * 512].rearrange("p (o r u) -> p o r u", o=2, u=2),
-                    bank[:].rearrange("p (o u r) -> p o r u", o=2, u=2),
-                )
-            return grp
+        grp_now = [None]
+        bank_now = [None]
+        turned = [0]
 
-        def quantise_chunk(grp):
-            codes = gq.tile([P, 4 * P], U32, name="g_codes", align_bytes=64)
-            scales = gq.tile([P, 4 * P], U8, name="g_scales", align_bytes=64)
-            nc.vector.quantize_mx(out=codes[:].bitcast(E5M2X4), scales=scales[:], in_=grp[:])
-            return codes, scales
+        def turn(count):
+            for k_ in range(count):
+                n = turned[0]
+                turned[0] += 1
+                if n % 8 == 0:
+                    grp_now[0] = gwork.tile([P, 4 * K_PASS], BF16, name="grp", align_bytes=64)
+                if n % 4 == 0:
+                    bank_now[0] = psum.tile([P, 512], F32, name="tp", tag="bank%d" % (HEAD + n // 4 % 4 if n < 32 else LATE_BANKS[(n // 4 - 8) % len(LATE_BANKS)]))
+                i, c = STREAM[n // 2]
+                nc.tensor.transpose(
+                    bank_now[0][:, n % 4 * P:(n % 4 + 1) * P], src[(i, c)][:, n % 2 * P:(n % 2 + 1) * P], ident[:])
+                if n % 4 == 3:
+                    half = n // 4 % 2
+                    copy(
+                        ENGINES[n // 4 % len(ENGINES)] if n >= B_FROM else LOW_ENGINES[n // 4 % len(LOW_ENGINES)] if n >= 32 else HEAD_ENGINES[n // 4 % 2],
+                        grp_now[0][:].bitcast(F32)[:, half * 512:(half + 1) * 512].rearrange("p (o r u) -> p o r u", o=2, u=2),
+                        bank_now[0][:].rearrange("p (o u r) -> p o r u", o=2, u=2),
+                    )
+                if n % 8 == 7:
+                    waiting.append((n // 8, grp_now[0]))
+
+        def quantise_waiting():
+            for n, grp in waiting:
+                codes = gq.tile([P, 4 * P], U32, name="g_codes", align_bytes=64)
+                scales = gq.tile([P, 4 * P], U8, name="g_scales", align_bytes=64)
+                nc.vector.quantize_mx(out=codes[:].bitcast(E5M2X4), scales=scales[:], in_=grp[:])
+                for j in range(4):
+                    ready.append((STREAM[4 * n + j], codes[:, j * P:(j + 1) * P], scales[:, j * P:(j + 1) * P]))
+            waiting.clear()
 
         def regroup_w(c):
             grp = wwork.tile([P, 4 * N], BF16, name="w_grp", align_bytes=64)
@@ -132,57 +148,56 @@ def tile_myinterleavedmodule_t_kernel(tc, x, weights, grad_out, out):
             nc.vector.quantize_mx(out=w_codes[c][:].bitcast(E4M3X4), scales=w_scales[c][:], in_=grp[:])
 
         def multiply(group):
-            for ops, codes, scales in group:
-                for j, (i, c) in enumerate(ops):
-                    if c % HALF == 0:
-                        acc[i] = psum.tile([P, N], F32, name="acc", tag="bank%d" % (acc_next[0] % HEAD))
-                        acc_next[0] += 1
-                    nc.tensor.matmul_mx(
-                        out=acc[i][:],
-                        lhsT=codes[:, j * P:(j + 1) * P].bitcast(E5M2X4),
-                        lhsT_scale=scales[:, j * P:(j + 1) * P],
-                        rhs=w_codes[c][:].bitcast(E4M3X4),
-                        rhs_scale=w_scales[c][:],
-                        start=(c % HALF == 0),
-                        stop=(c % HALF == HALF - 1),
-                    )
-                    if c == HALF - 1:
-                        part[i] = const.tile([P, N], F32, name="part%d" % i)
-                        nc.scalar.copy(out=part[i][:], in_=acc[i][:])
-                    if c == PASSES - 1:
-                        nc.vector.tensor_tensor(out=part[i][:], in0=acc[i][:], in1=part[i][:], op=ADD)
-                        nc.sync.dma_start(out=o[:, i, :], in_=part[i][:])
+            for (i, c), codes, scales in group:
+                opens = c == 0 or (c == HALF and i not in HELD)
+                closes = c == PASSES - 1 or (c == HALF - 1 and i not in HELD)
+                if opens:
+                    acc[i] = psum.tile([P, N], F32, name="acc", tag="bank%d" % (acc_next[0] % HEAD))
+                    acc_next[0] += 1
+                nc.tensor.matmul_mx(
+                    out=acc[i][:],
+                    lhsT=codes.bitcast(E5M2X4),
+                    lhsT_scale=scales,
+                    rhs=w_codes[c][:].bitcast(E4M3X4),
+                    rhs_scale=w_scales[c][:],
+                    start=opens,
+                    stop=closes,
+                )
+                if not closes:
+                    continue
+                if i in HELD:
+                    part[i] = const.tile([P, N], F32, name="part%d" % i)
+                    copy("s", part[i][:], acc[i][:])
+                elif c == HALF - 1:
+                    part[i] = const.tile([P, N], F32, name="part%d" % i)
+                    copy("v" if i in PART_V else "s", part[i][:], acc[i][:])
+                elif i == LAST:
+                    for cols in (slice(0, N // 2), slice(N // 2, N)):
+                        nc.vector.tensor_tensor(out=part[i][:, cols], in0=acc[i][:, cols], in1=part[i][:, cols], op=ADD)
+                        nc.sync.dma_start(out=o[:, i, cols], in_=part[i][:, cols])
+                else:
+                    nc.vector.tensor_tensor(out=part[i][:], in0=acc[i][:], in1=part[i][:], op=ADD)
+                if c == PASSES - 1 and i != LAST:
+                    nc.sync.dma_start(out=o[:, i, :], in_=part[i][:])
 
         def keep_warm(count):
+            if not count:
+                return
+            bank = psum.tile([P, 512], F32, name="warm", tag="bank0")
             for n in range(count):
-                bank = psum.tile([P, 512], F32, name="warm", tag="bank0")
                 nc.tensor.matmul(bank[:], lhsT=zeros[:, 0:P], rhs=zeros[:], start=True, stop=True)
 
-        def prepare_head(c):
-            ops = [(i, c) for i in range(HEAD)]
-            grp = transpose_and_copy(ops, "ss")
-            if c < len(WARM) - 1:
-                keep_warm(WARM[c + 1])
-            w_grp = regroup_w(c)
-            codes, scales = quantise_chunk(grp)
-            quantise_w(c, w_grp)
-            return [(ops, codes, scales)]
-
-        def prepare_pair(first, half, w_chunk):
-            chunks = [[(i, half * HALF + c) for c in range(HALF)] for i in range(first, first + PAIR)]
-            grps = [transpose_and_copy(chunks[0], "ss"), transpose_and_copy(chunks[1], "sv")]
-            w_grp = regroup_w(w_chunk) if w_chunk is not None else None
-            group = [(ops,) + quantise_chunk(grp) for ops, grp in zip(chunks, grps)]
-            if w_chunk is not None:
-                quantise_w(w_chunk, w_grp)
-            return group
+        def multiply_next(count):
+            multiply(ready[:count])
+            ready[:] = ready[count:]
 
         ident = const.tile([P, P], F32, name="ident")
         make_identity(nc, ident[:])
         zeros = const.tile([P, 512], BF16, name="zeros")
         nc.vector.memset(zeros[:], 0.0)
 
-        pairs = [(first, 0) for first in range(HEAD, TILES, PAIR)] + [(first, 1) for first in range(0, TILES, PAIR)]
+        pairs = [(first, 0) for first in range(HEAD, TILES, PAIR)]
+        pairs += [(first, 1) for first in [12, 14, 0, 2, 4, 6, 8, 10]]
         late_w_after = {2: 4, 3: 5, 4: 6, 5: 7}
 
         def load_next(n):
@@ -197,15 +212,42 @@ def tile_myinterleavedmodule_t_kernel(tc, x, weights, grad_out, out):
         for n in range(RING):
             load_next(n)
 
+        STREAM = [(i, c) for c in range(HALF) for i in range(HEAD)]
+        STREAM += [(i, half * HALF + c) for first, half in pairs for i in range(first, first + PAIR) for c in range(HALF)]
+        ENGINES = "s"
+        HEAD_ENGINES = "ss"
+        LATE_BANKS = (4, 5, 6, 7)
+        LOW_ENGINES = "ssv"
+        B_FROM = 128
+        R = 7
+        LAG = 3
+        ready = []
+        waiting = []
         keep_warm(WARM[0])
-        pending = prepare_head(0)
-        for c in range(1, HALF):
-            following = prepare_head(c)
-            multiply(pending)
-            pending = following
-        for n, (first, half) in enumerate(pairs):
-            following = prepare_pair(first, half, late_w_after.get(n - 1))
-            load_next(n + RING)
-            multiply(pending)
-            pending = following
-        multiply(pending)
+        total = len(STREAM)
+        made = 0
+        used = 0
+        loaded = 0
+        W_AT = {0: [0], 1: [1], 2: [2], 3: [3], 7: [4], 8: [5], 9: [6], 10: [7]}
+        SIZES = [4, 4, 4, 4, 8]
+        n = 0
+        while used < total:
+            before = made
+            size = min(SIZES[min(n, len(SIZES) - 1)], total - made)
+            turn(2 * size)
+            made += size
+            if n < len(WARM) - 1:
+                keep_warm(WARM[n + 1])
+            w_grps = [(c, regroup_w(c)) for c in W_AT.get(n, [])]
+            quantise_waiting()
+            for c, grp in w_grps:
+                quantise_w(c, grp)
+            while loaded < (made - 16) // 8:
+                load_next(loaded + RING)
+                loaded += 1
+            until = before // 4 * 4
+            if made == before:
+                until = total
+            multiply_next(max(0, until - used))
+            used = max(used, until)
+            n += 1

import concourse.mybir as mybir
from concourse.masks import make_identity

F32 = mybir.dt.float32
BF16 = mybir.dt.bfloat16
U32 = mybir.dt.uint32
U8 = mybir.dt.uint8
E5M2X4 = mybir.dt.float8_e5m2_x4
E4M3X4 = mybir.dt.float8_e4m3fn_x4
ADD = mybir.AluOpType.add

P = 128
TOKENS = 2048
K = 4096
N = 512
K_PASS = 512
PASSES = K // K_PASS
HALF = PASSES // 2
TILES = TOKENS // P
WORDS = K_PASS // 2
HEAD = 4
W_VECTOR_GROUPS = 80
RING = 6
PAIR = 2
HELD = (12, 13, 14, 15)
PART_V = ()
LAST = 11
WARM = (4, 3, 0)

FLOPS = 2 * TOKENS * K * N
BYTES = 2 * TOKENS * K + 2 * K * N + 4 * TOKENS * N


def tile_myinterleavedmodule_t_kernel(tc, x, weights, grad_out, out):
    nc = tc.nc
    g = grad_out.flatten_outer_dims().rearrange("(p i) k -> p i k", i=TILES)
    o = out.flatten_outer_dims().rearrange("(p i) n -> p i n", i=TILES)

    with tc.tile_pool(name="const", bufs=1) as const, \
            tc.tile_pool(name="raw", bufs=1) as raw, \
            tc.tile_pool(name="wwork", bufs=2) as wwork, \
            tc.tile_pool(name="gwork", bufs=6) as gwork, \
            tc.tile_pool(name="gq", bufs=9) as gq, \
            tc.tile_pool(name="gring", bufs=RING) as gring, \
            tc.psum_pool(name="psum", bufs=1) as psum, \
            tc.manual_schedule():

        src = {}
        w_raw = {}
        w_codes = {}
        w_scales = {}
        acc = {}
        part = {}
        tp_next = [0]
        acc_next = [0]

        def copy(engine, dst, source):
            if engine == "v":
                nc.vector.tensor_copy(out=dst, in_=source)
            else:
                nc.scalar.copy(out=dst, in_=source)

        def load_head(c):
            t = raw.tile([P, HEAD * K_PASS], BF16, name="g_head%d" % c)
            view = t[:].rearrange("p (i k) -> p i k", i=HEAD)
            step = HEAD // 2 if c == 0 else HEAD
            for j in range(0, HEAD, step):
                nc.sync.dma_start(
                    out=view[:, j:j + step],
                    in_=g[:, j:j + step, c * K_PASS:(c + 1) * K_PASS],
                )
            words = t[:].bitcast(F32)
            for i in range(HEAD):
                src[(i, c)] = words[:, i * WORDS:(i + 1) * WORDS]

        def load_pair(first, half, split):
            t = gring.tile([P, PAIR * HALF * K_PASS], BF16, name="g_pair")
            k0 = half * HALF * K_PASS
            width = HALF * K_PASS
            if split:
                for j in range(PAIR):
                    nc.sync.dma_start(out=t[:, j * width:(j + 1) * width], in_=g[:, first + j, k0:k0 + width])
            else:
                nc.sync.dma_start(
                    out=t[:].rearrange("p (i k) -> p i k", i=PAIR),
                    in_=g[:, first:first + PAIR, k0:k0 + width],
                )
            words = t[:].bitcast(F32)
            for j in range(PAIR):
                for c in range(HALF):
                    base = (j * HALF + c) * WORDS
                    src[(first + j, half * HALF + c)] = words[:, base:base + WORDS]

        def load_w(c):
            t = raw.tile([P, 4 * N], BF16, name="w_raw%d" % c)
            nc.sync.dma_start(
                out=t[:].rearrange("p (u e n) -> p u e n", u=2, e=2),
                in_=weights[c * K_PASS:(c + 1) * K_PASS, :].rearrange("(u p e) n -> p u e n", u=2, e=2),
            )
            w_raw[c] = t

        grp_now = [None]
        bank_now = [None]
        turned = [0]

        def turn(count):
            for k_ in range(count):
                n = turned[0]
                turned[0] += 1
                if n % 8 == 0:
                    grp_now[0] = gwork.tile([P, 4 * K_PASS], BF16, name="grp", align_bytes=64)
                if n % 4 == 0:
                    bank_now[0] = psum.tile([P, 512], F32, name="tp", tag="bank%d" % (HEAD + n // 4 % 4 if n < 32 else LATE_BANKS[(n // 4 - 8) % len(LATE_BANKS)]))
                i, c = STREAM[n // 2]
                nc.tensor.transpose(
                    bank_now[0][:, n % 4 * P:(n % 4 + 1) * P], src[(i, c)][:, n % 2 * P:(n % 2 + 1) * P], ident[:])
                if n % 4 == 3:
                    half = n // 4 % 2
                    copy(
                        ENGINES[n // 4 % len(ENGINES)] if n >= B_FROM else LOW_ENGINES[n // 4 % len(LOW_ENGINES)] if n >= 32 else HEAD_ENGINES[n // 4 % 2],
                        grp_now[0][:].bitcast(F32)[:, half * 512:(half + 1) * 512].rearrange("p (o r u) -> p o r u", o=2, u=2),
                        bank_now[0][:].rearrange("p (o u r) -> p o r u", o=2, u=2),
                    )
                if n % 8 == 7:
                    waiting.append((n // 8, grp_now[0]))

        def quantise_waiting():
            for n, grp in waiting:
                codes = gq.tile([P, 4 * P], U32, name="g_codes", align_bytes=64)
                scales = gq.tile([P, 4 * P], U8, name="g_scales", align_bytes=64)
                nc.vector.quantize_mx(out=codes[:].bitcast(E5M2X4), scales=scales[:], in_=grp[:])
                for j in range(4):
                    ready.append((STREAM[4 * n + j], codes[:, j * P:(j + 1) * P], scales[:, j * P:(j + 1) * P]))
            waiting.clear()

        def regroup_w(c):
            grp = wwork.tile([P, 4 * N], BF16, name="w_grp", align_bytes=64)
            dst = grp[:].rearrange("p (c i t) -> p c t i", i=4, t=4)
            source = w_raw[c][:].rearrange("p (t c i) -> p c t i", t=4, i=4)
            v = W_VECTOR_GROUPS
            nc.vector.tensor_copy(out=dst[:, 0:v], in_=source[:, 0:v])
            nc.scalar.copy(out=dst[:, v:], in_=source[:, v:])
            return grp

        def quantise_w(c, grp):
            w_codes[c] = const.tile([P, N], U32, name="w_codes%d" % c, align_bytes=64)
            w_scales[c] = const.tile([P, N], U8, name="w_scales%d" % c, align_bytes=64)
            nc.vector.quantize_mx(out=w_codes[c][:].bitcast(E4M3X4), scales=w_scales[c][:], in_=grp[:])

        def multiply(group):
            for (i, c), codes, scales in group:
                opens = c == 0 or (c == HALF and i not in HELD)
                closes = c == PASSES - 1 or (c == HALF - 1 and i not in HELD)
                if opens:
                    acc[i] = psum.tile([P, N], F32, name="acc", tag="bank%d" % (acc_next[0] % HEAD))
                    acc_next[0] += 1
                nc.tensor.matmul_mx(
                    out=acc[i][:],
                    lhsT=codes.bitcast(E5M2X4),
                    lhsT_scale=scales,
                    rhs=w_codes[c][:].bitcast(E4M3X4),
                    rhs_scale=w_scales[c][:],
                    start=opens,
                    stop=closes,
                )
                if not closes:
                    continue
                if i in HELD:
                    part[i] = const.tile([P, N], F32, name="part%d" % i)
                    copy("s", part[i][:], acc[i][:])
                elif c == HALF - 1:
                    part[i] = const.tile([P, N], F32, name="part%d" % i)
                    copy("v" if i in PART_V else "s", part[i][:], acc[i][:])
                elif i == LAST:
                    for cols in (slice(0, N // 2), slice(N // 2, N)):
                        nc.vector.tensor_tensor(out=part[i][:, cols], in0=acc[i][:, cols], in1=part[i][:, cols], op=ADD)
                        nc.sync.dma_start(out=o[:, i, cols], in_=part[i][:, cols])
                else:
                    nc.vector.tensor_tensor(out=part[i][:], in0=acc[i][:], in1=part[i][:], op=ADD)
                if c == PASSES - 1 and i != LAST:
                    nc.sync.dma_start(out=o[:, i, :], in_=part[i][:])

        def keep_warm(count):
            if not count:
                return
            bank = psum.tile([P, 512], F32, name="warm", tag="bank0")
            for n in range(count):
                nc.tensor.matmul(bank[:], lhsT=zeros[:, 0:P], rhs=zeros[:], start=True, stop=True)

        def multiply_next(count):
            multiply(ready[:count])
            ready[:] = ready[count:]

        ident = const.tile([P, P], F32, name="ident")
        make_identity(nc, ident[:])
        zeros = const.tile([P, 512], BF16, name="zeros")
        nc.vector.memset(zeros[:], 0.0)

        pairs = [(first, 0) for first in range(HEAD, TILES, PAIR)]
        pairs += [(first, 1) for first in [12, 14, 0, 2, 4, 6, 8, 10]]
        late_w_after = {2: 4, 3: 5, 4: 6, 5: 7}

        def load_next(n):
            if n < len(pairs):
                load_pair(pairs[n][0], pairs[n][1], n < 2)
                if n in late_w_after:
                    load_w(late_w_after[n])

        for c in range(HALF):
            load_head(c)
            load_w(c)
        for n in range(RING):
            load_next(n)

        STREAM = [(i, c) for c in range(HALF) for i in range(HEAD)]
        STREAM += [(i, half * HALF + c) for first, half in pairs for i in range(first, first + PAIR) for c in range(HALF)]
        ENGINES = "s"
        HEAD_ENGINES = "ss"
        LATE_BANKS = (4, 5, 6, 7)
        LOW_ENGINES = "ssv"
        B_FROM = 128
        R = 7
        LAG = 3
        ready = []
        waiting = []
        keep_warm(WARM[0])
        total = len(STREAM)
        made = 0
        used = 0
        loaded = 0
        W_AT = {0: [0], 1: [1], 2: [2], 3: [3], 7: [4], 8: [5], 9: [6], 10: [7]}
        SIZES = [4, 4, 4, 4, 8]
        n = 0
        while used < total:
            before = made
            size = min(SIZES[min(n, len(SIZES) - 1)], total - made)
            turn(2 * size)
            made += size
            if n < len(WARM) - 1:
                keep_warm(WARM[n + 1])
            w_grps = [(c, regroup_w(c)) for c in W_AT.get(n, [])]
            quantise_waiting()
            for c, grp in w_grps:
                quantise_w(c, grp)
            while loaded < (made - 16) // 8:
                load_next(loaded + RING)
                loaded += 1
            until = before // 4 * 4
            if made == before:
                until = total
            multiply_next(max(0, until - used))
            used = max(used, until)
            n += 1
